import numpy as np
import ml_dtypes


def mxq(x, axis, fmt="e4m3"):
    dtype, down = {"e4m3": (ml_dtypes.float8_e4m3fn, 7), "e5m2": (ml_dtypes.float8_e5m2, 14)}[fmt]
    v = np.moveaxis(np.asarray(x, np.float32).astype(ml_dtypes.bfloat16).astype(np.float64), axis, -1)
    blocks = v.reshape(v.shape[:-1] + (-1, 32))
    amax = np.abs(blocks).max(-1, keepdims=True)
    byte = np.maximum(np.where(amax > 0, np.frexp(amax)[1] - 1 + 127, 0) - down, 1)
    scale = np.exp2(byte - 127.0)
    codes = (blocks / scale).astype(np.float32).astype(dtype).astype(np.float64)
    return np.moveaxis((codes * scale).reshape(v.shape), -1, axis)


WIDE = False


def mx_kscale(k):
    if not WIDE:
        return np.ones(k)
    levels = np.array([10, -10, 5, -5, 0])
    if k % 512:
        return np.exp2(np.random.permutation(np.resize(levels, k // 32))).repeat(32)
    a = np.empty((k // 512, 16))
    for p in range(k // 512):
        a[p, :8] = np.random.permutation(np.resize(levels, 8))
        for g in range(8):
            far = levels[np.abs(levels - a[p, g]) >= 10]
            a[p, g + 8] = far[np.random.randint(len(far))]
    return np.exp2(a.ravel()).repeat(32)


BF16 = ml_dtypes.bfloat16


def bf(x):
    return np.asarray(x, np.float32).astype(BF16)


def f64(x):
    return np.asarray(x).astype(np.float64)


B, C, V, K, OUT = 16, 128, 1024, 4, 128


def setup_inputs():
    s = mx_kscale(V)
    g = np.random.standard_normal((V, V))
    lap = (g + g.T) * (0.45 / np.sqrt(V))
    return {"input": bf(np.random.standard_normal((B, C, V)) * s),
            "laplacian": bf(lap * s[:, None] / s[None, :])}


def reference(input, laplacian):
    x0 = f64(input).transpose(2, 1, 0).reshape(V, C * B)
    lq = mxq(f64(laplacian), 1, "e4m3")
    x1 = lq @ mxq(x0, 0, "e4m3")
    x2 = 2.0 * (lq @ mxq(x1, 0, "e4m3")) - x0
    return x1, x2

@@ -1,0 +1,272 @@
+from contextlib import ExitStack
+
+import concourse.mybir as mybir
+from concourse.masks import make_identity
+
+F32 = mybir.dt.float32
+BF16 = mybir.dt.bfloat16
+U32 = mybir.dt.uint32
+U8 = mybir.dt.uint8
+FP8X4 = mybir.dt.float8_e4m3fn_x4
+ALU = mybir.AluOpType
+
+P = 128
+V = 1024
+N = 2048
+FLOPS = 2 * 2 * V * V * N
+
+PIECES = (4, 4, 4, 2, 2)
+LAP_AT = (1, 1)
+WARM = (0, 3, 0, 3, 0, 0, 1, 2)
+SG = (9, 12, 15, 18, 21, 24, 27)
+
+
+def tile_graph_conv_pa_t_kernel(tc, signal, laplacian, out_0, out_1):
+    nc = tc.nc
+    with ExitStack() as ctx:
+        keep = ctx.enter_context(tc.tile_pool(name="keep", bufs=1))
+        big = ctx.enter_context(tc.tile_pool(name="big", bufs=4))
+        lgp = ctx.enter_context(tc.tile_pool(name="lgp", bufs=2))
+        x2p = ctx.enter_context(tc.tile_pool(name="x2p", bufs=6))
+        x1gp = ctx.enter_context(tc.tile_pool(name="x1gp", bufs=3))
+        psum = ctx.enter_context(tc.psum_pool(name="psum", bufs=8))
+        ctx.enter_context(tc.manual_schedule())
+
+        ident = keep.tile([P, P], F32, name="ident")
+        make_identity(nc, ident[:])
+        zeros = keep.tile([P, 512], BF16, name="zeros")
+        nc.vector.memset(zeros[:], 0.0)
+
+        lraw = [keep.tile([P, 2048], BF16, name="lraw%d" % a) for a in range(4)]
+        xraw = [big.tile([P, 8192], BF16, name="xraw%d" % i, tag="big") for i in range(2)]
+        x0g = [keep.tile([P, 4 * N], BF16, name="x0g%d" % g, align_bytes=64) for g in range(2)]
+        x0c = keep.tile([P, 2 * N], U32, name="x0c", align_bytes=64)
+        x0s = keep.tile([P, 2 * N], U8, name="x0s", align_bytes=64)
+        x1c = keep.tile([P, 2 * N], U32, name="x1c", align_bytes=64)
+        x1s = keep.tile([P, 2 * N], U8, name="x1s", align_bytes=64)
+        lc = keep.tile([P, 2048], U32, name="lc", align_bytes=64)
+        ls = keep.tile([P, 2048], U8, name="ls", align_bytes=64)
+
+        lap_rows = laplacian.rearrange("(gp p uh e) u -> gp uh p (e u)", gp=2, p=P, uh=2, e=2)
+        sig_rows = signal.rearrange("b (h r) v -> (b h) (r v)", h=8, r=16)
+
+        def load_lap(a):
+            nc.sync.dma_start(out=lraw[a][:], in_=lap_rows[a // 2, a % 2])
+
+        load_lap(0)
+        r0 = 0
+        for nr in PIECES:
+            half, rl = r0 // 8, r0 % 8
+            nc.sync.dma_start(out=xraw[half][:, rl * 1024:(rl + nr) * 1024], in_=sig_rows[:, r0 * 1024:(r0 + nr) * 1024])
+            r0 += nr
+        for a in range(1, 4):
+            load_lap(a)
+
+        out_views = [o.rearrange("(gp p uh e) n -> gp uh p e n", gp=2, p=P, uh=2, e=2) for o in (out_0, out_1)]
+
+        def new_bank():
+            bank = psum.tile([P, 512], F32, name="bank", tag="bank")
+            return bank
+
+        def warm(count):
+            bank = new_bank()
+            for rep in range(count):
+                nc.tensor.matmul(out=bank[:], lhsT=zeros[:, 0:P], rhs=zeros[:], start=True, stop=True)
+
+        lgs = {}
+
+        def lap_bank(a, g):
+            bank = new_bank()
+            words = lraw[a][:].bitcast(F32)
+            for u in range(2):
+                for e in range(2):
+                    off = e * 512 + g * 256 + u
+                    slot = 2 * u + e
+                    nc.tensor.transpose(out=bank[:, slot * P:(slot + 1) * P], in_=words[:, off:off + 255:2], identity=ident[:])
+            return bank
+
+        def lap_copy(copy, a, g, bank):
+            if g == 0:
+                lg = lgp.tile([P, 2048], BF16, name="lg", tag="lg", align_bytes=64)
+                lgs[a] = lg
+            dst = lgs[a][:].bitcast(F32)[:, g * 512:(g + 1) * 512].rearrange("q (x u) -> q x u", u=2)
+            src = bank[:].rearrange("q (u x) -> q x u", u=2)
+            copy(out=dst, in_=src)
+
+        def lap_quant(a):
+            nc.vector.quantize_mx(
+                out=lc[:, a * 512:(a + 1) * 512].bitcast(FP8X4),
+                scales=ls[:, a * 512:(a + 1) * 512],
+                in_=lgs[a][:],
+            )
+
+        def x_bank(k, g):
+            bank = new_bank()
+            for u in range(2):
+                for rr in range(2):
+                    r = 2 * k + rr
+                    words = xraw[r // 8][:].bitcast(F32)
+                    off = (r % 8) * 512 + g * 256 + u
+                    slot = 2 * u + rr
+                    nc.tensor.transpose(out=bank[:, slot * P:(slot + 1) * P], in_=words[:, off:off + 255:2], identity=ident[:])
+            return bank
+
+        def x_copy(copy, k, g, bank):
+            dst = x0g[g][:].bitcast(F32).rearrange("q (h x u) -> q h x u", h=8, x=256, u=2)[:, :, 32 * k:32 * k + 32, :]
+            src = bank[:].rearrange("q (u x h) -> q h x u", u=2, x=32, h=8)
+            copy(out=dst, in_=src)
+
+        def x_quant(j, hs):
+            for h in hs:
+                for g in range(2):
+                    c0 = h * 256 + j * 64
+                    nc.vector.quantize_mx(
+                        out=x0c[:, g * N + c0:g * N + c0 + 64].bitcast(FP8X4),
+                        scales=x0s[:, g * N + c0:g * N + c0 + 64],
+                        in_=x0g[g][:, 4 * c0:4 * c0 + 256],
+                    )
+
+        def mx_pass(bank, a, e, g, codes, scales, ch):
+            w = a * 512 + g * 256 + e * P
+            c = g * N + ch * 512
+            nc.tensor.matmul_mx(
+                out=bank[:],
+                lhsT=lc[:, w:w + P].bitcast(FP8X4),
+                lhsT_scale=ls[:, w:w + P],
+                rhs=codes[:, c:c + 512].bitcast(FP8X4),
+                rhs_scale=scales[:, c:c + 512],
+                start=(g == 0),
+                stop=(g == 1),
+            )
+
+        s_copy = nc.scalar.copy
+        v_copy = nc.vector.tensor_copy
+
+        ALL_H = tuple(range(8))
+        warm(4)
+        b0 = lap_bank(0, 0)
+        lap_copy(s_copy, 0, 0, b0)
+        b1 = lap_bank(0, 1)
+        lap_copy(v_copy, 0, 1, b1)
+        lap_quant(0)
+        warm(3)
+        for k in range(8):
+            for g in range(2):
+                bank = x_bank(k, g)
+                on_vector = (g == 0 and k in (1, 3, 5)) or (g == 1 and k in (6, 7))
+                x_copy(v_copy if on_vector else s_copy, k, g, bank)
+            if k == 1:
+                x_quant(0, ALL_H)
+            if k == 3:
+                x_quant(1, ALL_H)
+            if k == 6:
+                x_quant(2, (0, 1))
+            if WARM[k] > 0:
+                warm(WARM[k])
+        x_quant(3, (0, 1))
+        for ch in range(1, 4):
+            for j in (2, 3):
+                x_quant(j, (2 * ch, 2 * ch + 1))
+            if ch == 1:
+                for g in range(2):
+                    bank = lap_bank(1, g)
+                    lap_copy(s_copy, 1, g, bank)
+                lap_quant(1)
+
+        x1sb = {}
+        x1g = {}
+
+        def s1_tasks(gp, ch, ts):
+            key = (gp, ch // 2)
+            if key not in x1sb:
+                pair = big.tile([P, 4096], F32, name="pair", tag="big")
+                x1sb[key] = pair
+            for t in ts:
+                bank = new_bank()
+                for g in range(2):
+                    mx_pass(bank, 2 * gp + t // 2, t % 2, g, x0c, x0s, ch)
+                c = t * 1024 + (ch % 2) * 512
+                nc.scalar.copy(out=x1sb[key][:, c:c + 512], in_=bank[:])
+
+        def s1_store(gp, uh, c0, c1):
+            half = c0 // 1024
+            src = x1sb[(gp, half)][:, uh * 2048:(uh + 1) * 2048].rearrange("p (e n) -> p e n", e=2)
+            nc.sync.dma_start(out=out_views[0][gp, uh][:, :, c0:c1], in_=src[:, :, c0 - half * 1024:c1 - half * 1024])
+
+        def s1_store_row(gp, t, half):
+            nc.sync.dma_start(
+                out=out_views[0][gp, t // 2][:, t % 2, half * 1024:(half + 1) * 1024],
+                in_=x1sb[(gp, half)][:, t * 1024:(t + 1) * 1024],
+            )
+
+        def regroup(gp, ch, copy):
+            xg = x1gp.tile([P, 2048], BF16, name="xg", tag="xg", align_bytes=64)
+            x1g[(gp, ch)] = xg
+            src = x1sb[(gp, ch // 2)][:].rearrange("p (t n) -> p t n", t=4)[:, :, (ch % 2) * 512:(ch % 2) * 512 + 512]
+            copy(
+                out=xg[:].rearrange("p (c i t) -> p c t i", c=P, i=4, t=4),
+                in_=src.rearrange("p t (c i) -> p c t i", c=P, i=4),
+            )
+
+        def x1_quant(gp, ch):
+            c = gp * N + ch * 512
+            nc.vector.quantize_mx(out=x1c[:, c:c + 512].bitcast(FP8X4), scales=x1s[:, c:c + 512], in_=x1g[(gp, ch)][:])
+
+        def lap_late():
+            for a in (2, 3):
+                bank = lap_bank(a, 0)
+                lap_copy(s_copy, a, 0, bank)
+                bank = lap_bank(a, 1)
+                lap_copy(v_copy, a, 1, bank)
+            lap_quant(2)
+            lap_quant(3)
+
+        pairs = [(0, 0), (0, 1), (1, 0), (1, 1)]
+        for i, (gp, half) in enumerate(pairs):
+            for t in range(4):
+                for cc in range(2):
+                    s1_tasks(gp, 2 * half + cc, (t,))
+                s1_store_row(gp, t, half)
+                if i == LAP_AT[0] and t == LAP_AT[1]:
+                    lap_late()
+            if i < 3:
+                for cc in range(2):
+                    regroup(gp, 2 * half + cc, v_copy)
+                for cc in range(2):
+                    x1_quant(gp, 2 * half + cc)
+
+        def s2_evict(i, mt, ch, bank, res):
+            a, e = mt // 2, mt % 2
+            t = 2 * (a % 2) + e
+            x0t = x0g[a // 2][:].rearrange("q (n t) -> q n t", t=4)[:, ch * 512:(ch + 1) * 512, t]
+            if i in SG:
+                nc.scalar.mul(out=res, in_=bank[:], mul=2.0)
+                nc.gpsimd.tensor_tensor(out=res, in0=res, in1=x0t, op=ALU.subtract)
+            else:
+                nc.vector.scalar_tensor_tensor(out=res, in0=bank[:], scalar=2.0, in1=x0t, op0=ALU.mult, op1=ALU.subtract)
+
+        def s2_store(mt, xt, half, c0, c1):
+            a, e = mt // 2, mt % 2
+            nc.sync.dma_start(out=out_views[1][a // 2, a % 2][:, e, half * 1024 + c0:half * 1024 + c1], in_=xt[:, c0:c1])
+
+        regroup(1, 2, s_copy)
+        regroup(1, 3, s_copy)
+        i = 0
+        for half in range(2):
+            for mt in range(8):
+                xt = x2p.tile([P, 1024], F32, name="xt", tag="xt")
+                for cc in range(2):
+                    ch = 2 * half + cc
+                    bank = new_bank()
+                    for g in range(2):
+                        mx_pass(bank, mt // 2, mt % 2, g, x1c, x1s, ch)
+                    s2_evict(i, mt, ch, bank, xt[:, cc * 512:(cc + 1) * 512])
+                    i += 1
+                    if half == 1 and mt == 7:
+                        s2_store(mt, xt, half, cc * 512, (cc + 1) * 512)
+                if not (half == 1 and mt == 7):
+                    s2_store(mt, xt, half, 0, 1024)
+                if half == 0 and mt == 3:
+                    x1_quant(1, 2)
+                if half == 0 and mt == 5:
+                    x1_quant(1, 3)

@@ -15,19 +15,13 @@ V = 1024
 N = 2048
 FLOPS = 2 * 2 * V * V * N
 
-PIECES = (4, 4, 4, 2, 2)
-LAP_AT = (1, 1)
-WARM = (0, 3, 0, 3, 0, 0, 1, 2)
-SG = (9, 12, 15, 18, 21, 24, 27)
-
 
 def tile_graph_conv_pa_t_kernel(tc, signal, laplacian, out_0, out_1):
     nc = tc.nc
     with ExitStack() as ctx:
         keep = ctx.enter_context(tc.tile_pool(name="keep", bufs=1))
-        big = ctx.enter_context(tc.tile_pool(name="big", bufs=4))
+        big = ctx.enter_context(tc.tile_pool(name="big", bufs=5))
         lgp = ctx.enter_context(tc.tile_pool(name="lgp", bufs=2))
-        x2p = ctx.enter_context(tc.tile_pool(name="x2p", bufs=6))
         x1gp = ctx.enter_context(tc.tile_pool(name="x1gp", bufs=3))
         psum = ctx.enter_context(tc.psum_pool(name="psum", bufs=8))
         ctx.enter_context(tc.manual_schedule())
@@ -38,7 +32,7 @@ def tile_graph_conv_pa_t_kernel(tc, signal, laplacian, out_0, out_1):
         nc.vector.memset(zeros[:], 0.0)
 
         lraw = [keep.tile([P, 2048], BF16, name="lraw%d" % a) for a in range(4)]
-        xraw = [big.tile([P, 8192], BF16, name="xraw%d" % i, tag="big") for i in range(2)]
+        xraw = [keep.tile([P, 4096], BF16, name="xraw%d" % i) for i in range(4)]
         x0g = [keep.tile([P, 4 * N], BF16, name="x0g%d" % g, align_bytes=64) for g in range(2)]
         x0c = keep.tile([P, 2 * N], U32, name="x0c", align_bytes=64)
         x0s = keep.tile([P, 2 * N], U8, name="x0s", align_bytes=64)
@@ -48,21 +42,29 @@ def tile_graph_conv_pa_t_kernel(tc, signal, laplacian, out_0, out_1):
         ls = keep.tile([P, 2048], U8, name="ls", align_bytes=64)
 
         lap_rows = laplacian.rearrange("(gp p uh e) u -> gp uh p (e u)", gp=2, p=P, uh=2, e=2)
-        sig_rows = signal.rearrange("b (h r) v -> (b h) (r v)", h=8, r=16)
+        sig_rows = signal.rearrange("b (ch h r) v -> ch b h (r v)", ch=4, h=8, r=4)
 
         def load_lap(a):
             nc.sync.dma_start(out=lraw[a][:], in_=lap_rows[a // 2, a % 2])
 
-        load_lap(0)
-        r0 = 0
-        for nr in PIECES:
-            half, rl = r0 // 8, r0 % 8
-            nc.sync.dma_start(out=xraw[half][:, rl * 1024:(rl + nr) * 1024], in_=sig_rows[:, r0 * 1024:(r0 + nr) * 1024])
-            r0 += nr
-        for a in range(1, 4):
-            load_lap(a)
+        def load_x(ch, c0, c1):
+            nc.sync.dma_start(out=xraw[ch][:, c0:c1], in_=sig_rows[ch][:, :, c0:c1])
 
-        out_views = [o.rearrange("(gp p uh e) n -> gp uh p e n", gp=2, p=P, uh=2, e=2) for o in (out_0, out_1)]
+        load_lap(0)
+        load_lap(1)
+        load_x(0, 0, 2048)
+        load_x(0, 2048, 4096)
+        load_x(1, 0, 2048)
+        load_x(1, 2048, 4096)
+        load_lap(2)
+        load_lap(3)
+        load_x(2, 0, 4096)
+        load_x(3, 0, 4096)
+
+        out_views = [o.rearrange("(gp p t) n -> gp t p n", gp=2, p=P, t=4) for o in (out_0, out_1)]
+
+        s_copy = nc.scalar.copy
+        v_copy = nc.vector.tensor_copy
 
         def new_bank():
             bank = psum.tile([P, 512], F32, name="bank", tag="bank")
@@ -73,25 +75,22 @@ def tile_graph_conv_pa_t_kernel(tc, signal, laplacian, out_0, out_1):
             for rep in range(count):
                 nc.tensor.matmul(out=bank[:], lhsT=zeros[:, 0:P], rhs=zeros[:], start=True, stop=True)
 
-        lgs = {}
-
-        def lap_bank(a, g):
+        def transposes(raw, offsets):
             bank = new_bank()
-            words = lraw[a][:].bitcast(F32)
-            for u in range(2):
-                for e in range(2):
-                    off = e * 512 + g * 256 + u
-                    slot = 2 * u + e
-                    nc.tensor.transpose(out=bank[:, slot * P:(slot + 1) * P], in_=words[:, off:off + 255:2], identity=ident[:])
+            words = raw[:].bitcast(F32)
+            for slot, off in enumerate(offsets):
+                nc.tensor.transpose(out=bank[:, slot * P:(slot + 1) * P], in_=words[:, off:off + 255:2], identity=ident[:])
             return bank
 
-        def lap_copy(copy, a, g, bank):
-            if g == 0:
-                lg = lgp.tile([P, 2048], BF16, name="lg", tag="lg", align_bytes=64)
-                lgs[a] = lg
-            dst = lgs[a][:].bitcast(F32)[:, g * 512:(g + 1) * 512].rearrange("q (x u) -> q x u", u=2)
-            src = bank[:].rearrange("q (u x) -> q x u", u=2)
-            copy(out=dst, in_=src)
+        lgs = {}
+
+        def lap_turn(a, copies):
+            lg = lgp.tile([P, 2048], BF16, name="lg", tag="lg", align_bytes=64)
+            lgs[a] = lg
+            for g in range(2):
+                bank = transposes(lraw[a], [e * 512 + g * 256 + u for u in range(2) for e in range(2)])
+                dst = lg[:].bitcast(F32)[:, g * 512:(g + 1) * 512].rearrange("q (x u) -> q x u", u=2)
+                copies[g](out=dst, in_=bank[:].rearrange("q (u x) -> q x u", u=2))
 
         def lap_quant(a):
             nc.vector.quantize_mx(
@@ -100,106 +99,57 @@ def tile_graph_conv_pa_t_kernel(tc, signal, laplacian, out_0, out_1):
                 in_=lgs[a][:],
             )
 
-        def x_bank(k, g):
-            bank = new_bank()
-            for u in range(2):
-                for rr in range(2):
-                    r = 2 * k + rr
-                    words = xraw[r // 8][:].bitcast(F32)
-                    off = (r % 8) * 512 + g * 256 + u
-                    slot = 2 * u + rr
-                    nc.tensor.transpose(out=bank[:, slot * P:(slot + 1) * P], in_=words[:, off:off + 255:2], identity=ident[:])
-            return bank
-
-        def x_copy(copy, k, g, bank):
-            dst = x0g[g][:].bitcast(F32).rearrange("q (h x u) -> q h x u", h=8, x=256, u=2)[:, :, 32 * k:32 * k + 32, :]
-            src = bank[:].rearrange("q (u x h) -> q h x u", u=2, x=32, h=8)
-            copy(out=dst, in_=src)
-
-        def x_quant(j, hs):
-            for h in hs:
-                for g in range(2):
-                    c0 = h * 256 + j * 64
-                    nc.vector.quantize_mx(
-                        out=x0c[:, g * N + c0:g * N + c0 + 64].bitcast(FP8X4),
-                        scales=x0s[:, g * N + c0:g * N + c0 + 64],
-                        in_=x0g[g][:, 4 * c0:4 * c0 + 256],
-                    )
-
-        def mx_pass(bank, a, e, g, codes, scales, ch):
-            w = a * 512 + g * 256 + e * P
-            c = g * N + ch * 512
-            nc.tensor.matmul_mx(
-                out=bank[:],
-                lhsT=lc[:, w:w + P].bitcast(FP8X4),
-                lhsT_scale=ls[:, w:w + P],
-                rhs=codes[:, c:c + 512].bitcast(FP8X4),
-                rhs_scale=scales[:, c:c + 512],
-                start=(g == 0),
-                stop=(g == 1),
-            )
-
-        s_copy = nc.scalar.copy
-        v_copy = nc.vector.tensor_copy
-
-        ALL_H = tuple(range(8))
-        warm(4)
-        b0 = lap_bank(0, 0)
-        lap_copy(s_copy, 0, 0, b0)
-        b1 = lap_bank(0, 1)
-        lap_copy(v_copy, 0, 1, b1)
-        lap_quant(0)
-        warm(3)
-        for k in range(8):
+        def x_turn(ch, k, copies):
             for g in range(2):
-                bank = x_bank(k, g)
-                on_vector = (g == 0 and k in (1, 3, 5)) or (g == 1 and k in (6, 7))
-                x_copy(v_copy if on_vector else s_copy, k, g, bank)
-            if k == 1:
-                x_quant(0, ALL_H)
-            if k == 3:
-                x_quant(1, ALL_H)
-            if k == 6:
-                x_quant(2, (0, 1))
-            if WARM[k] > 0:
-                warm(WARM[k])
-        x_quant(3, (0, 1))
-        for ch in range(1, 4):
-            for j in (2, 3):
-                x_quant(j, (2 * ch, 2 * ch + 1))
-            if ch == 1:
-                for g in range(2):
-                    bank = lap_bank(1, g)
-                    lap_copy(s_copy, 1, g, bank)
-                lap_quant(1)
+                bank = transposes(xraw[ch], [(2 * k + rr) * 512 + g * 256 + u for u in range(2) for rr in range(2)])
+                dst = x0g[g][:].bitcast(F32)[:, ch * 1024:(ch + 1) * 1024]
+                dst = dst.rearrange("q (h x u) -> q h x u", h=8, x=64, u=2)[:, :, 32 * k:32 * k + 32, :]
+                copies[g](out=dst, in_=bank[:].rearrange("q (u x h) -> q h x u", u=2, x=32, h=8))
+
+        def x_quant(ch):
+            for g in range(2):
+                c = g * N + ch * 512
+                nc.vector.quantize_mx(
+                    out=x0c[:, c:c + 512].bitcast(FP8X4),
+                    scales=x0s[:, c:c + 512],
+                    in_=x0g[g][:, ch * 2048:(ch + 1) * 2048],
+                )
+
+        def product(codes, scales, mt, ch):
+            bank = new_bank()
+            for g in range(2):
+                w = (mt // 2) * 512 + g * 256 + (mt % 2) * P
+                c = g * N + ch * 512
+                nc.tensor.matmul_mx(
+                    out=bank[:],
+                    lhsT=lc[:, w:w + P].bitcast(FP8X4),
+                    lhsT_scale=ls[:, w:w + P],
+                    rhs=codes[:, c:c + 512].bitcast(FP8X4),
+                    rhs_scale=scales[:, c:c + 512],
+                    start=(g == 0),
+                    stop=(g == 1),
+                )
+            return bank
 
         x1sb = {}
         x1g = {}
 
-        def s1_tasks(gp, ch, ts):
+        def s1(gp, t, ch, copy=s_copy):
             key = (gp, ch // 2)
             if key not in x1sb:
                 pair = big.tile([P, 4096], F32, name="pair", tag="big")
                 x1sb[key] = pair
-            for t in ts:
-                bank = new_bank()
-                for g in range(2):
-                    mx_pass(bank, 2 * gp + t // 2, t % 2, g, x0c, x0s, ch)
-                c = t * 1024 + (ch % 2) * 512
-                nc.scalar.copy(out=x1sb[key][:, c:c + 512], in_=bank[:])
+            bank = product(x0c, x0s, 4 * gp + t, ch)
+            c = t * 1024 + (ch % 2) * 512
+            copy(out=x1sb[key][:, c:c + 512], in_=bank[:])
 
-        def s1_store(gp, uh, c0, c1):
-            half = c0 // 1024
-            src = x1sb[(gp, half)][:, uh * 2048:(uh + 1) * 2048].rearrange("p (e n) -> p e n", e=2)
-            nc.sync.dma_start(out=out_views[0][gp, uh][:, :, c0:c1], in_=src[:, :, c0 - half * 1024:c1 - half * 1024])
-
-        def s1_store_row(gp, t, half):
+        def s1_store(gp, t, half):
             nc.sync.dma_start(
-                out=out_views[0][gp, t // 2][:, t % 2, half * 1024:(half + 1) * 1024],
+                out=out_views[0][gp, t][:, half * 1024:(half + 1) * 1024],
                 in_=x1sb[(gp, half)][:, t * 1024:(t + 1) * 1024],
             )
 
-        def regroup(gp, ch, copy):
+        def regroup(gp, ch, copy=v_copy):
             xg = x1gp.tile([P, 2048], BF16, name="xg", tag="xg", align_bytes=64)
             x1g[(gp, ch)] = xg
             src = x1sb[(gp, ch // 2)][:].rearrange("p (t n) -> p t n", t=4)[:, :, (ch % 2) * 512:(ch % 2) * 512 + 512]
@@ -212,61 +162,116 @@ def tile_graph_conv_pa_t_kernel(tc, signal, laplacian, out_0, out_1):
             c = gp * N + ch * 512
             nc.vector.quantize_mx(out=x1c[:, c:c + 512].bitcast(FP8X4), scales=x1s[:, c:c + 512], in_=x1g[(gp, ch)][:])
 
-        def lap_late():
-            for a in (2, 3):
-                bank = lap_bank(a, 0)
-                lap_copy(s_copy, a, 0, bank)
-                bank = lap_bank(a, 1)
-                lap_copy(v_copy, a, 1, bank)
-            lap_quant(2)
-            lap_quant(3)
-
-        pairs = [(0, 0), (0, 1), (1, 0), (1, 1)]
-        for i, (gp, half) in enumerate(pairs):
-            for t in range(4):
-                for cc in range(2):
-                    s1_tasks(gp, 2 * half + cc, (t,))
-                s1_store_row(gp, t, half)
-                if i == LAP_AT[0] and t == LAP_AT[1]:
-                    lap_late()
-            if i < 3:
-                for cc in range(2):
-                    regroup(gp, 2 * half + cc, v_copy)
-                for cc in range(2):
-                    x1_quant(gp, 2 * half + cc)
-
-        def s2_evict(i, mt, ch, bank, res):
-            a, e = mt // 2, mt % 2
-            t = 2 * (a % 2) + e
-            x0t = x0g[a // 2][:].rearrange("q (n t) -> q n t", t=4)[:, ch * 512:(ch + 1) * 512, t]
-            if i in SG:
+        def s2(mt, ch, res, scalar_path):
+            bank = product(x1c, x1s, mt, ch)
+            x0t = x0g[mt // 4][:].rearrange("q (n t) -> q n t", t=4)[:, ch * 512:(ch + 1) * 512, mt % 4]
+            if scalar_path:
                 nc.scalar.mul(out=res, in_=bank[:], mul=2.0)
                 nc.gpsimd.tensor_tensor(out=res, in0=res, in1=x0t, op=ALU.subtract)
             else:
                 nc.vector.scalar_tensor_tensor(out=res, in0=bank[:], scalar=2.0, in1=x0t, op0=ALU.mult, op1=ALU.subtract)
 
-        def s2_store(mt, xt, half, c0, c1):
-            a, e = mt // 2, mt % 2
-            nc.sync.dma_start(out=out_views[1][a // 2, a % 2][:, e, half * 1024 + c0:half * 1024 + c1], in_=xt[:, c0:c1])
+        SV = (s_copy, v_copy)
+
+        SS = (s_copy, s_copy)
+        warm(4)
+        lap_turn(0, SV)
+        warm(1)
+        lap_turn(1, SV)
+        warm(1)
+        lap_quant(0)
+        x_turn(0, 0, SV)
+        warm(1)
+        lap_quant(1)
+        x_turn(0, 1, SV)
+        warm(1)
+        x_quant(0)
+        x_turn(1, 0, SS)
+
+        for t in (0, 1):
+            s1(0, t, 0)
+        x_turn(1, 1, (s_copy, v_copy))
+        x_quant(1)
+        for t in (2, 3):
+            s1(0, t, 0)
+        lap_turn(2, SV)
+        for t in (0, 1):
+            s1(0, t, 1)
+            s1_store(0, t, 0)
+        lap_turn(3, SV)
+        lap_quant(2)
+        lap_quant(3)
+        for t in (2, 3):
+            s1(0, t, 1)
+            s1_store(0, t, 0)
+        regroup(0, 0)
+        x_turn(2, 0, SV)
+        for ch in (0, 1):
+            s1(1, 0, ch)
+        s1_store(1, 0, 0)
+        x_turn(2, 1, SV)
+        x_quant(2)
+        for ch in (0, 1):
+            s1(1, 1, ch)
+        s1_store(1, 1, 0)
+        x1_quant(0, 0)
+        x_turn(3, 0, SV)
+        regroup(0, 1)
+        for ch in (0, 1):
+            s1(1, 2, ch)
+        s1_store(1, 2, 0)
+        x_turn(3, 1, SV)
+        x_quant(3)
+        for ch in (0, 1):
+            s1(1, 3, ch)
+        s1_store(1, 3, 0)
+        x1_quant(0, 1)
+
+        regroup(1, 0)
+        for ch in (2, 3):
+            for t in (0, 1):
+                s1(0, t, ch)
+        for t in (0, 1):
+            s1_store(0, t, 1)
+        regroup(1, 1)
+        x1_quant(1, 0)
+        for t in (2, 3):
+            for ch in (2, 3):
+                s1(0, t, ch)
+            s1_store(0, t, 1)
+        x1_quant(1, 1)
+        regroup(0, 2)
+        regroup(0, 3)
+        x1_quant(0, 2)
+        x1_quant(0, 3)
+        for t in range(4):
+            for ch in (2, 3):
+                s1(1, t, ch)
+            s1_store(1, t, 1)
 
         regroup(1, 2, s_copy)
         regroup(1, 3, s_copy)
         i = 0
         for half in range(2):
-            for mt in range(8):
-                xt = x2p.tile([P, 1024], F32, name="xt", tag="xt")
-                for cc in range(2):
-                    ch = 2 * half + cc
-                    bank = new_bank()
-                    for g in range(2):
-                        mx_pass(bank, mt // 2, mt % 2, g, x1c, x1s, ch)
-                    s2_evict(i, mt, ch, bank, xt[:, cc * 512:(cc + 1) * 512])
-                    i += 1
-                    if half == 1 and mt == 7:
-                        s2_store(mt, xt, half, cc * 512, (cc + 1) * 512)
-                if not (half == 1 and mt == 7):
-                    s2_store(mt, xt, half, 0, 1024)
-                if half == 0 and mt == 3:
-                    x1_quant(1, 2)
-                if half == 0 and mt == 5:
-                    x1_quant(1, 3)
+            for gp in range(2):
+                pair = big.tile([P, 4096], F32, name="pair", tag="big")
+                for t in range(4):
+                    mt = 4 * gp + t
+                    for cc in range(2):
+                        c = t * 1024 + cc * 512
+                        s2(mt, 2 * half + cc, pair[:, c:c + 512], i % 4 == 2 and i >= 8 and i < 30)
+                        i += 1
+                        if half == 1 and mt == 7:
+                            nc.sync.dma_start(
+                                out=out_views[1][gp, t][:, 1024 + cc * 512:1536 + cc * 512],
+                                in_=pair[:, c:c + 512],
+                            )
+                    if not (half == 1 and mt == 7):
+                        nc.sync.dma_start(
+                            out=out_views[1][gp, t][:, half * 1024:(half + 1) * 1024],
+                            in_=pair[:, t * 1024:(t + 1) * 1024],
+                        )
+                    if half == 0 and mt == 3:
+                        x1_quant(1, 2)
+                    if half == 0 and mt == 5:
+                        x1_quant(1, 3)

@@ -52,14 +52,14 @@ def tile_graph_conv_pa_t_kernel(tc, signal, laplacian, out_0, out_1):
 
         load_lap(0)
         load_lap(1)
-        load_x(0, 0, 2048)
-        load_x(0, 2048, 4096)
-        load_x(1, 0, 2048)
-        load_x(1, 2048, 4096)
+        for ch in range(2):
+            for r in range(4):
+                load_x(ch, r * 1024, (r + 1) * 1024)
         load_lap(2)
         load_lap(3)
-        load_x(2, 0, 4096)
-        load_x(3, 0, 4096)
+        for ch in range(2, 4):
+            for r in range(4):
+                load_x(ch, r * 1024, (r + 1) * 1024)
 
         out_views = [o.rearrange("(gp p t) n -> gp t p n", gp=2, p=P, t=4) for o in (out_0, out_1)]
 

@@ -20,9 +20,10 @@ def tile_graph_conv_pa_t_kernel(tc, signal, laplacian, out_0, out_1):
     nc = tc.nc
     with ExitStack() as ctx:
         keep = ctx.enter_context(tc.tile_pool(name="keep", bufs=1))
-        big = ctx.enter_context(tc.tile_pool(name="big", bufs=5))
+        big = ctx.enter_context(tc.tile_pool(name="big", bufs=4))
         lgp = ctx.enter_context(tc.tile_pool(name="lgp", bufs=2))
         x1gp = ctx.enter_context(tc.tile_pool(name="x1gp", bufs=3))
+        permp = ctx.enter_context(tc.tile_pool(name="permp", bufs=3))
         psum = ctx.enter_context(tc.psum_pool(name="psum", bufs=8))
         ctx.enter_context(tc.manual_schedule())
 
@@ -75,20 +76,32 @@ def tile_graph_conv_pa_t_kernel(tc, signal, laplacian, out_0, out_1):
             for rep in range(count):
                 nc.tensor.matmul(out=bank[:], lhsT=zeros[:, 0:P], rhs=zeros[:], start=True, stop=True)
 
-        def transposes(raw, offsets):
+        def even_odd(raw, c0, copy):
+            perm = permp.tile([P, 1024], F32, name="perm", tag="perm")
+            src = raw[:, 2 * c0:2 * c0 + 2048].bitcast(F32).rearrange("p (s q u) -> p s u q", s=4, q=P, u=2)
+            copy(out=perm[:].rearrange("p (s u q) -> p s u q", s=4, q=P, u=2), in_=src)
+            return perm
+
+        def transposes(perm, g):
             bank = new_bank()
-            words = raw[:].bitcast(F32)
-            for slot, off in enumerate(offsets):
-                nc.tensor.transpose(out=bank[:, slot * P:(slot + 1) * P], in_=words[:, off:off + 255:2], identity=ident[:])
+            for slot in range(4):
+                u, e = slot // 2, slot % 2
+                off = e * 512 + g * 256 + u * P
+                nc.tensor.transpose(out=bank[:, slot * P:(slot + 1) * P], in_=perm[:, off:off + P], identity=ident[:])
             return bank
 
         lgs = {}
+
+        perms = {}
+
+        def lap_perm(a, copy=v_copy):
+            perms[a] = even_odd(lraw[a], 0, copy)
 
         def lap_turn(a, copies):
             lg = lgp.tile([P, 2048], BF16, name="lg", tag="lg", align_bytes=64)
             lgs[a] = lg
             for g in range(2):
-                bank = transposes(lraw[a], [e * 512 + g * 256 + u for u in range(2) for e in range(2)])
+                bank = transposes(perms[a], g)
                 dst = lg[:].bitcast(F32)[:, g * 512:(g + 1) * 512].rearrange("q (x u) -> q x u", u=2)
                 copies[g](out=dst, in_=bank[:].rearrange("q (u x) -> q x u", u=2))
 
@@ -99,9 +112,12 @@ def tile_graph_conv_pa_t_kernel(tc, signal, laplacian, out_0, out_1):
                 in_=lgs[a][:],
             )
 
+        def x_perm(ch, k, copy=v_copy):
+            perms[(ch, k)] = even_odd(xraw[ch], k * 1024, copy)
+
         def x_turn(ch, k, copies):
             for g in range(2):
-                bank = transposes(xraw[ch], [(2 * k + rr) * 512 + g * 256 + u for u in range(2) for rr in range(2)])
+                bank = transposes(perms[(ch, k)], g)
                 dst = x0g[g][:].bitcast(F32)[:, ch * 1024:(ch + 1) * 1024]
                 dst = dst.rearrange("q (h x u) -> q h x u", h=8, x=64, u=2)[:, :, 32 * k:32 * k + 32, :]
                 copies[g](out=dst, in_=bank[:].rearrange("q (u x h) -> q h x u", u=2, x=32, h=8))
@@ -175,53 +191,65 @@ def tile_graph_conv_pa_t_kernel(tc, signal, laplacian, out_0, out_1):
 
         SS = (s_copy, s_copy)
         warm(4)
-        lap_turn(0, SV)
-        warm(1)
-        lap_turn(1, SV)
-        warm(1)
+        lap_perm(0)
+        lap_turn(0, SS)
+        warm(2)
+        lap_perm(1)
+        lap_turn(1, SS)
+        warm(2)
+        x_perm(0, 0)
         lap_quant(0)
-        x_turn(0, 0, SV)
-        warm(1)
+        x_turn(0, 0, SS)
+        warm(2)
+        x_perm(0, 1)
         lap_quant(1)
-        x_turn(0, 1, SV)
-        warm(1)
+        x_turn(0, 1, SS)
+        warm(2)
+        x_perm(1, 0)
         x_quant(0)
         x_turn(1, 0, SS)
 
+        x_perm(1, 1)
         for t in (0, 1):
             s1(0, t, 0)
-        x_turn(1, 1, (s_copy, v_copy))
+        x_turn(1, 1, SS)
+        lap_perm(2)
         x_quant(1)
         for t in (2, 3):
             s1(0, t, 0)
+        lap_perm(3)
         lap_turn(2, SV)
         for t in (0, 1):
             s1(0, t, 1)
             s1_store(0, t, 0)
+        x_perm(2, 0)
         lap_turn(3, SV)
         lap_quant(2)
         lap_quant(3)
         for t in (2, 3):
             s1(0, t, 1)
             s1_store(0, t, 0)
-        regroup(0, 0)
+        x_perm(2, 1)
         x_turn(2, 0, SV)
+        x_perm(3, 0)
         for ch in (0, 1):
             s1(1, 0, ch)
         s1_store(1, 0, 0)
         x_turn(2, 1, SV)
+        x_perm(3, 1)
         x_quant(2)
+        regroup(0, 0)
         for ch in (0, 1):
             s1(1, 1, ch)
         s1_store(1, 1, 0)
-        x1_quant(0, 0)
         x_turn(3, 0, SV)
-        regroup(0, 1)
         for ch in (0, 1):
             s1(1, 2, ch)
         s1_store(1, 2, 0)
+        x1_quant(0, 0)
         x_turn(3, 1, SV)
         x_quant(3)
+        regroup(0, 1)
         for ch in (0, 1):
             s1(1, 3, ch)
         s1_store(1, 3, 0)

@@ -23,7 +23,6 @@ def tile_graph_conv_pa_t_kernel(tc, signal, laplacian, out_0, out_1):
         big = ctx.enter_context(tc.tile_pool(name="big", bufs=4))
         lgp = ctx.enter_context(tc.tile_pool(name="lgp", bufs=2))
         x1gp = ctx.enter_context(tc.tile_pool(name="x1gp", bufs=3))
-        permp = ctx.enter_context(tc.tile_pool(name="permp", bufs=3))
         psum = ctx.enter_context(tc.psum_pool(name="psum", bufs=8))
         ctx.enter_context(tc.manual_schedule())
 
@@ -33,7 +32,7 @@ def tile_graph_conv_pa_t_kernel(tc, signal, laplacian, out_0, out_1):
         nc.vector.memset(zeros[:], 0.0)
 
         lraw = [keep.tile([P, 2048], BF16, name="lraw%d" % a) for a in range(4)]
-        xraw = [keep.tile([P, 4096], BF16, name="xraw%d" % i) for i in range(4)]
+        xraw = [keep.tile([P, 8192], BF16, name="xraw%d" % i) for i in range(2)]
         x0g = [keep.tile([P, 4 * N], BF16, name="x0g%d" % g, align_bytes=64) for g in range(2)]
         x0c = keep.tile([P, 2 * N], U32, name="x0c", align_bytes=64)
         x0s = keep.tile([P, 2 * N], U8, name="x0s", align_bytes=64)
@@ -43,24 +42,20 @@ def tile_graph_conv_pa_t_kernel(tc, signal, laplacian, out_0, out_1):
         ls = keep.tile([P, 2048], U8, name="ls", align_bytes=64)
 
         lap_rows = laplacian.rearrange("(gp p uh e) u -> gp uh p (e u)", gp=2, p=P, uh=2, e=2)
-        sig_rows = signal.rearrange("b (ch h r) v -> ch b h (r v)", ch=4, h=8, r=4)
+        sig_rows = signal.rearrange("b (h r) v -> (b h) (r v)", h=8, r=16)
 
         def load_lap(a):
             nc.sync.dma_start(out=lraw[a][:], in_=lap_rows[a // 2, a % 2])
 
-        def load_x(ch, c0, c1):
-            nc.sync.dma_start(out=xraw[ch][:, c0:c1], in_=sig_rows[ch][:, :, c0:c1])
+        def load_x(k):
+            c = (k % 4) * 2048
+            nc.sync.dma_start(out=xraw[k // 4][:, c:c + 2048], in_=sig_rows[:, k * 2048:(k + 1) * 2048])
 
         load_lap(0)
-        load_lap(1)
-        for ch in range(2):
-            for r in range(4):
-                load_x(ch, r * 1024, (r + 1) * 1024)
-        load_lap(2)
-        load_lap(3)
-        for ch in range(2, 4):
-            for r in range(4):
-                load_x(ch, r * 1024, (r + 1) * 1024)
+        for k in range(8):
+            load_x(k)
+        for a in range(1, 4):
+            load_lap(a)
 
         out_views = [o.rearrange("(gp p t) n -> gp t p n", gp=2, p=P, t=4) for o in (out_0, out_1)]
 
@@ -76,32 +71,22 @@ def tile_graph_conv_pa_t_kernel(tc, signal, laplacian, out_0, out_1):
             for rep in range(count):
                 nc.tensor.matmul(out=bank[:], lhsT=zeros[:, 0:P], rhs=zeros[:], start=True, stop=True)
 
-        def even_odd(raw, c0, copy):
-            perm = permp.tile([P, 1024], F32, name="perm", tag="perm")
-            src = raw[:, 2 * c0:2 * c0 + 2048].bitcast(F32).rearrange("p (s q u) -> p s u q", s=4, q=P, u=2)
-            copy(out=perm[:].rearrange("p (s u q) -> p s u q", s=4, q=P, u=2), in_=src)
-            return perm
-
-        def transposes(perm, g):
+        def transposes(raw, c0, g):
             bank = new_bank()
+            words = raw[:].bitcast(F32)
             for slot in range(4):
                 u, e = slot // 2, slot % 2
-                off = e * 512 + g * 256 + u * P
-                nc.tensor.transpose(out=bank[:, slot * P:(slot + 1) * P], in_=perm[:, off:off + P], identity=ident[:])
+                off = c0 + e * 512 + g * 256 + u
+                nc.tensor.transpose(out=bank[:, slot * P:(slot + 1) * P], in_=words[:, off:off + 255:2], identity=ident[:])
             return bank
 
         lgs = {}
-
-        perms = {}
-
-        def lap_perm(a, copy=v_copy):
-            perms[a] = even_odd(lraw[a], 0, copy)
 
         def lap_turn(a, copies):
             lg = lgp.tile([P, 2048], BF16, name="lg", tag="lg", align_bytes=64)
             lgs[a] = lg
             for g in range(2):
-                bank = transposes(perms[a], g)
+                bank = transposes(lraw[a], 0, g)
                 dst = lg[:].bitcast(F32)[:, g * 512:(g + 1) * 512].rearrange("q (x u) -> q x u", u=2)
                 copies[g](out=dst, in_=bank[:].rearrange("q (u x) -> q x u", u=2))
 
@@ -112,30 +97,27 @@ def tile_graph_conv_pa_t_kernel(tc, signal, laplacian, out_0, out_1):
                 in_=lgs[a][:],
             )
 
-        def x_perm(ch, k, copy=v_copy):
-            perms[(ch, k)] = even_odd(xraw[ch], k * 1024, copy)
-
-        def x_turn(ch, k, copies):
+        def x_turn(k, copies):
             for g in range(2):
-                bank = transposes(perms[(ch, k)], g)
-                dst = x0g[g][:].bitcast(F32)[:, ch * 1024:(ch + 1) * 1024]
-                dst = dst.rearrange("q (h x u) -> q h x u", h=8, x=64, u=2)[:, :, 32 * k:32 * k + 32, :]
+                bank = transposes(xraw[k // 4], (k % 4) * 1024, g)
+                dst = x0g[g][:].bitcast(F32).rearrange("q (f h x u) -> q f h x u", f=2, h=8, x=128, u=2)[:, k // 4]
+                dst = dst[:, :, 32 * (k % 4):32 * (k % 4) + 32, :]
                 copies[g](out=dst, in_=bank[:].rearrange("q (u x h) -> q h x u", u=2, x=32, h=8))
 
-        def x_quant(ch):
+        def x_quant(f, hq):
             for g in range(2):
-                c = g * N + ch * 512
+                c = g * N + f * 1024 + hq * 512
                 nc.vector.quantize_mx(
                     out=x0c[:, c:c + 512].bitcast(FP8X4),
                     scales=x0s[:, c:c + 512],
-                    in_=x0g[g][:, ch * 2048:(ch + 1) * 2048],
+                    in_=x0g[g][:, f * 4096 + hq * 2048:f * 4096 + hq * 2048 + 2048],
                 )
 
-        def product(codes, scales, mt, ch):
+        def product(codes, scales, mt, f, hq):
             bank = new_bank()
             for g in range(2):
                 w = (mt // 2) * 512 + g * 256 + (mt % 2) * P
-                c = g * N + ch * 512
+                c = g * N + f * 1024 + hq * 512
                 nc.tensor.matmul_mx(
                     out=bank[:],
                     lhsT=lc[:, w:w + P].bitcast(FP8X4),
@@ -147,159 +129,127 @@ def tile_graph_conv_pa_t_kernel(tc, signal, laplacian, out_0, out_1):
                 )
             return bank
 
+        def runs(tile, t, f):
+            return tile[:, t * 1024:(t + 1) * 1024].rearrange("p (h f x) -> p f h x", h=4, f=2, x=P)[:, f]
+
         x1sb = {}
         x1g = {}
 
-        def s1(gp, t, ch, copy=s_copy):
-            key = (gp, ch // 2)
+        def s1(gp, t, f, hq, copy=s_copy):
+            key = (gp, hq)
             if key not in x1sb:
                 pair = big.tile([P, 4096], F32, name="pair", tag="big")
                 x1sb[key] = pair
-            bank = product(x0c, x0s, 4 * gp + t, ch)
-            c = t * 1024 + (ch % 2) * 512
-            copy(out=x1sb[key][:, c:c + 512], in_=bank[:])
+            bank = product(x0c, x0s, 4 * gp + t, f, hq)
+            copy(out=runs(x1sb[key], t, f), in_=bank[:].rearrange("p (h x) -> p h x", h=4))
 
-        def s1_store(gp, t, half):
+        def s1_store(gp, t, hq):
             nc.sync.dma_start(
-                out=out_views[0][gp, t][:, half * 1024:(half + 1) * 1024],
-                in_=x1sb[(gp, half)][:, t * 1024:(t + 1) * 1024],
+                out=out_views[0][gp, t][:, hq * 1024:(hq + 1) * 1024],
+                in_=x1sb[(gp, hq)][:, t * 1024:(t + 1) * 1024],
             )
 
-        def regroup(gp, ch, copy=v_copy):
+        def regroup(gp, f, hq, copy=v_copy):
             xg = x1gp.tile([P, 2048], BF16, name="xg", tag="xg", align_bytes=64)
-            x1g[(gp, ch)] = xg
-            src = x1sb[(gp, ch // 2)][:].rearrange("p (t n) -> p t n", t=4)[:, :, (ch % 2) * 512:(ch % 2) * 512 + 512]
-            copy(
-                out=xg[:].rearrange("p (c i t) -> p c t i", c=P, i=4, t=4),
-                in_=src.rearrange("p t (c i) -> p c t i", c=P, i=4),
-            )
+            x1g[(gp, f, hq)] = xg
+            src = x1sb[(gp, hq)][:].rearrange("p (t h f c i) -> p f h c t i", t=4, h=4, f=2, c=32, i=4)[:, f]
+            copy(out=xg[:].rearrange("p (h c i t) -> p h c t i", h=4, c=32, i=4, t=4), in_=src)
 
-        def x1_quant(gp, ch):
-            c = gp * N + ch * 512
-            nc.vector.quantize_mx(out=x1c[:, c:c + 512].bitcast(FP8X4), scales=x1s[:, c:c + 512], in_=x1g[(gp, ch)][:])
+        def x1_quant(gp, f, hq):
+            c = gp * N + f * 1024 + hq * 512
+            nc.vector.quantize_mx(out=x1c[:, c:c + 512].bitcast(FP8X4), scales=x1s[:, c:c + 512], in_=x1g[(gp, f, hq)][:])
 
-        def s2(mt, ch, res, scalar_path):
-            bank = product(x1c, x1s, mt, ch)
-            x0t = x0g[mt // 4][:].rearrange("q (n t) -> q n t", t=4)[:, ch * 512:(ch + 1) * 512, mt % 4]
+        def s2(mt, f, hq, pair, scalar_path):
+            bank = product(x1c, x1s, mt, f, hq)
+            src = bank[:].rearrange("p (h x) -> p h x", h=4)
+            x0t = x0g[mt // 4][:].rearrange("q (n t) -> q n t", t=4)[:, f * 1024 + hq * 512:f * 1024 + hq * 512 + 512, mt % 4]
+            x0t = x0t.rearrange("q (h x) -> q h x", h=4)
+            res = runs(pair, mt % 4, f)
             if scalar_path:
-                nc.scalar.mul(out=res, in_=bank[:], mul=2.0)
+                nc.scalar.mul(out=res, in_=src, mul=2.0)
                 nc.gpsimd.tensor_tensor(out=res, in0=res, in1=x0t, op=ALU.subtract)
             else:
-                nc.vector.scalar_tensor_tensor(out=res, in0=bank[:], scalar=2.0, in1=x0t, op0=ALU.mult, op1=ALU.subtract)
+                nc.vector.scalar_tensor_tensor(out=res, in0=src, scalar=2.0, in1=x0t, op0=ALU.mult, op1=ALU.subtract)
+
+        def s2_store(mt, hq, pair):
+            nc.sync.dma_start(
+                out=out_views[1][mt // 4, mt % 4][:, hq * 1024:(hq + 1) * 1024],
+                in_=pair[:, (mt % 4) * 1024:(mt % 4 + 1) * 1024],
+            )
 
         SV = (s_copy, v_copy)
 
         SS = (s_copy, s_copy)
         warm(4)
-        lap_perm(0)
-        lap_turn(0, SS)
-        warm(2)
-        lap_perm(1)
+        lap_turn(0, SV)
+        warm(1)
+        for k in range(4):
+            x_turn(k, SV)
+            if k == 0:
+                lap_quant(0)
+            warm(1)
+        x_quant(0, 0)
+        x_turn(4, SS)
+        for t in (0, 1):
+            s1(0, t, 0, 0)
+        x_quant(0, 1)
+        x_turn(5, SV)
+        for t in (0, 1):
+            s1(0, t, 0, 1)
+        x_turn(6, SV)
+        x_turn(7, SV)
+        x_quant(1, 0)
         lap_turn(1, SS)
-        warm(2)
-        x_perm(0, 0)
-        lap_quant(0)
-        x_turn(0, 0, SS)
-        warm(2)
-        x_perm(0, 1)
+
         lap_quant(1)
-        x_turn(0, 1, SS)
-        warm(2)
-        x_perm(1, 0)
-        x_quant(0)
-        x_turn(1, 0, SS)
-
-        x_perm(1, 1)
         for t in (0, 1):
-            s1(0, t, 0)
-        x_turn(1, 1, SS)
-        lap_perm(2)
-        x_quant(1)
-        for t in (2, 3):
-            s1(0, t, 0)
-        lap_perm(3)
+            s1(0, t, 1, 0)
+            s1_store(0, t, 0)
+        x_quant(1, 1)
         lap_turn(2, SV)
-        for t in (0, 1):
-            s1(0, t, 1)
-            s1_store(0, t, 0)
-        x_perm(2, 0)
-        lap_turn(3, SV)
         lap_quant(2)
-        lap_quant(3)
         for t in (2, 3):
-            s1(0, t, 1)
+            for f in range(2):
+                s1(0, t, f, 0)
             s1_store(0, t, 0)
-        x_perm(2, 1)
-        x_turn(2, 0, SV)
-        x_perm(3, 0)
-        for ch in (0, 1):
-            s1(1, 0, ch)
-        s1_store(1, 0, 0)
-        x_turn(2, 1, SV)
-        x_perm(3, 1)
-        x_quant(2)
-        regroup(0, 0)
-        for ch in (0, 1):
-            s1(1, 1, ch)
-        s1_store(1, 1, 0)
-        x_turn(3, 0, SV)
-        for ch in (0, 1):
-            s1(1, 2, ch)
-        s1_store(1, 2, 0)
-        x1_quant(0, 0)
-        x_turn(3, 1, SV)
-        x_quant(3)
-        regroup(0, 1)
-        for ch in (0, 1):
-            s1(1, 3, ch)
-        s1_store(1, 3, 0)
-        x1_quant(0, 1)
-
-        regroup(1, 0)
-        for ch in (2, 3):
-            for t in (0, 1):
-                s1(0, t, ch)
-        for t in (0, 1):
-            s1_store(0, t, 1)
-        regroup(1, 1)
-        x1_quant(1, 0)
-        for t in (2, 3):
-            for ch in (2, 3):
-                s1(0, t, ch)
-            s1_store(0, t, 1)
-        x1_quant(1, 1)
-        regroup(0, 2)
-        regroup(0, 3)
-        x1_quant(0, 2)
-        x1_quant(0, 3)
+        lap_turn(3, SV)
+        lap_quant(3)
         for t in range(4):
-            for ch in (2, 3):
-                s1(1, t, ch)
-            s1_store(1, t, 1)
+            for f in range(2):
+                if t > 1 or f == 1:
+                    s1(0, t, f, 1)
+            s1_store(0, t, 1)
+            if t == 0:
+                regroup(0, 0, 0)
+            if t == 2:
+                regroup(0, 1, 0)
+                x1_quant(0, 0, 0)
+        x1_quant(0, 1, 0)
+        for hq in range(2):
+            for t in range(4):
+                for f in range(2):
+                    s1(1, t, f, hq)
+                s1_store(1, t, hq)
+                if t == 0:
+                    regroup(hq, 0, 1 - hq)
+                if t == 2:
+                    regroup(hq, 1, 1 - hq)
+                    x1_quant(hq, 0, 1 - hq)
+            x1_quant(hq, 1, 1 - hq)
 
-        regroup(1, 2, s_copy)
-        regroup(1, 3, s_copy)
+        regroup(1, 0, 1, s_copy)
+        regroup(1, 1, 1, s_copy)
         i = 0
-        for half in range(2):
+        for hq in range(2):
             for gp in range(2):
                 pair = big.tile([P, 4096], F32, name="pair", tag="big")
                 for t in range(4):
                     mt = 4 * gp + t
-                    for cc in range(2):
-                        c = t * 1024 + cc * 512
-                        s2(mt, 2 * half + cc, pair[:, c:c + 512], i % 4 == 2 and i >= 8 and i < 30)
+                    for f in range(2):
+                        s2(mt, f, hq, pair, i % 4 == 2 and i >= 8 and i < 30)
                         i += 1
-                        if half == 1 and mt == 7:
-                            nc.sync.dma_start(
-                                out=out_views[1][gp, t][:, 1024 + cc * 512:1536 + cc * 512],
-                                in_=pair[:, c:c + 512],
-                            )
-                    if not (half == 1 and mt == 7):
-                        nc.sync.dma_start(
-                            out=out_views[1][gp, t][:, half * 1024:(half + 1) * 1024],
-                            in_=pair[:, t * 1024:(t + 1) * 1024],
-                        )
-                    if half == 0 and mt == 3:
-                        x1_quant(1, 2)
-                    if half == 0 and mt == 5:
-                        x1_quant(1, 3)
+                    s2_store(mt, hq, pair)
+                    if hq == 0 and mt == 3:
+                        x1_quant(1, 0, 1)
+                    if hq == 0 and mt == 5:
+                        x1_quant(1, 1, 1)

@@ -113,17 +113,17 @@ def tile_graph_conv_pa_t_kernel(tc, signal, laplacian, out_0, out_1):
                     in_=x0g[g][:, f * 4096 + hq * 2048:f * 4096 + hq * 2048 + 2048],
                 )
 
-        def product(codes, scales, mt, f, hq):
+        def product(codes, scales, mt, c0, width):
             bank = new_bank()
             for g in range(2):
                 w = (mt // 2) * 512 + g * 256 + (mt % 2) * P
-                c = g * N + f * 1024 + hq * 512
+                c = g * N + c0
                 nc.tensor.matmul_mx(
-                    out=bank[:],
+                    out=bank[:, 0:width],
                     lhsT=lc[:, w:w + P].bitcast(FP8X4),
                     lhsT_scale=ls[:, w:w + P],
-                    rhs=codes[:, c:c + 512].bitcast(FP8X4),
-                    rhs_scale=scales[:, c:c + 512],
+                    rhs=codes[:, c:c + width].bitcast(FP8X4),
+                    rhs_scale=scales[:, c:c + width],
                     start=(g == 0),
                     stop=(g == 1),
                 )
@@ -140,7 +140,7 @@ def tile_graph_conv_pa_t_kernel(tc, signal, laplacian, out_0, out_1):
             if key not in x1sb:
                 pair = big.tile([P, 4096], F32, name="pair", tag="big")
                 x1sb[key] = pair
-            bank = product(x0c, x0s, 4 * gp + t, f, hq)
+            bank = product(x0c, x0s, 4 * gp + t, f * 1024 + hq * 512, 512)
             copy(out=runs(x1sb[key], t, f), in_=bank[:].rearrange("p (h x) -> p h x", h=4))
 
         def s1_store(gp, t, hq):
@@ -159,65 +159,58 @@ def tile_graph_conv_pa_t_kernel(tc, signal, laplacian, out_0, out_1):
             c = gp * N + f * 1024 + hq * 512
             nc.vector.quantize_mx(out=x1c[:, c:c + 512].bitcast(FP8X4), scales=x1s[:, c:c + 512], in_=x1g[(gp, f, hq)][:])
 
-        def s2(mt, f, hq, pair, scalar_path):
-            bank = product(x1c, x1s, mt, f, hq)
-            src = bank[:].rearrange("p (h x) -> p h x", h=4)
-            x0t = x0g[mt // 4][:].rearrange("q (n t) -> q n t", t=4)[:, f * 1024 + hq * 512:f * 1024 + hq * 512 + 512, mt % 4]
-            x0t = x0t.rearrange("q (h x) -> q h x", h=4)
-            res = runs(pair, mt % 4, f)
+        def s2(mt, f, hq, pair, scalar_path, h0=0, nh=4):
+            c = f * 1024 + hq * 512 + h0 * P
+            bank = product(x1c, x1s, mt, c, nh * P)
+            src = bank[:, 0:nh * P].rearrange("p (h x) -> p h x", h=nh)
+            x0t = x0g[mt // 4][:].rearrange("q (n t) -> q n t", t=4)[:, c:c + nh * P, mt % 4]
+            x0t = x0t.rearrange("q (h x) -> q h x", h=nh)
+            res = runs(pair, mt % 4, f)[:, h0:h0 + nh]
             if scalar_path:
                 nc.scalar.mul(out=res, in_=src, mul=2.0)
                 nc.gpsimd.tensor_tensor(out=res, in0=res, in1=x0t, op=ALU.subtract)
             else:
                 nc.vector.scalar_tensor_tensor(out=res, in0=src, scalar=2.0, in1=x0t, op0=ALU.mult, op1=ALU.subtract)
 
-        def s2_store(mt, hq, pair):
+        def s2_store(mt, hq, pair, c0=0, c1=1024):
+            t = mt % 4
             nc.sync.dma_start(
-                out=out_views[1][mt // 4, mt % 4][:, hq * 1024:(hq + 1) * 1024],
-                in_=pair[:, (mt % 4) * 1024:(mt % 4 + 1) * 1024],
+                out=out_views[1][mt // 4, t][:, hq * 1024 + c0:hq * 1024 + c1],
+                in_=pair[:, t * 1024 + c0:t * 1024 + c1],
             )
 
         SV = (s_copy, v_copy)
 
-        SS = (s_copy, s_copy)
         warm(4)
         lap_turn(0, SV)
-        warm(1)
-        for k in range(4):
+        for k in range(8):
             x_turn(k, SV)
             if k == 0:
                 lap_quant(0)
-            warm(1)
-        x_quant(0, 0)
-        x_turn(4, SS)
-        for t in (0, 1):
-            s1(0, t, 0, 0)
-        x_quant(0, 1)
-        x_turn(5, SV)
-        for t in (0, 1):
-            s1(0, t, 0, 1)
-        x_turn(6, SV)
-        x_turn(7, SV)
+            if k in (4, 5):
+                x_quant(0, k - 4)
+            if k % 2 == 0:
+                warm(1)
         x_quant(1, 0)
-        lap_turn(1, SS)
-
-        lap_quant(1)
-        for t in (0, 1):
-            s1(0, t, 1, 0)
-            s1_store(0, t, 0)
-        x_quant(1, 1)
+        lap_turn(1, (s_copy, s_copy))
         lap_turn(2, SV)
+        lap_quant(1)
+        x_quant(1, 1)
+
+        for t in (0, 1):
+            for f in range(2):
+                s1(0, t, f, 0)
+            s1_store(0, t, 0)
         lap_quant(2)
+        lap_turn(3, SV)
+        lap_quant(3)
         for t in (2, 3):
             for f in range(2):
                 s1(0, t, f, 0)
             s1_store(0, t, 0)
-        lap_turn(3, SV)
-        lap_quant(3)
         for t in range(4):
             for f in range(2):
-                if t > 1 or f == 1:
-                    s1(0, t, f, 1)
+                s1(0, t, f, 1)
             s1_store(0, t, 1)
             if t == 0:
                 regroup(0, 0, 0)
@@ -245,6 +238,12 @@ def tile_graph_conv_pa_t_kernel(tc, signal, laplacian, out_0, out_1):
                 pair = big.tile([P, 4096], F32, name="pair", tag="big")
                 for t in range(4):
                     mt = 4 * gp + t
+                    if (hq, mt) == (1, 7):
+                        for h0 in (0, 2):
+                            for f in range(2):
+                                s2(mt, f, hq, pair, False, h0, 2)
+                            s2_store(mt, hq, pair, h0 * 256, h0 * 256 + 512)
+                        break
                     for f in range(2):
                         s2(mt, f, hq, pair, i % 4 == 2 and i >= 8 and i < 30)
                         i += 1

@@ -23,6 +23,7 @@ def tile_graph_conv_pa_t_kernel(tc, signal, laplacian, out_0, out_1):
         big = ctx.enter_context(tc.tile_pool(name="big", bufs=4))
         lgp = ctx.enter_context(tc.tile_pool(name="lgp", bufs=2))
         x1gp = ctx.enter_context(tc.tile_pool(name="x1gp", bufs=3))
+        permp = ctx.enter_context(tc.tile_pool(name="permp", bufs=3))
         psum = ctx.enter_context(tc.psum_pool(name="psum", bufs=8))
         ctx.enter_context(tc.manual_schedule())
 
@@ -71,24 +72,41 @@ def tile_graph_conv_pa_t_kernel(tc, signal, laplacian, out_0, out_1):
             for rep in range(count):
                 nc.tensor.matmul(out=bank[:], lhsT=zeros[:, 0:P], rhs=zeros[:], start=True, stop=True)
 
-        def transposes(raw, c0, g):
+        def even_odd(raw, c0):
+            perm = permp.tile([P, 1024], F32, name="perm", tag="perm")
+            src = raw[:].bitcast(F32)[:, c0:c0 + 1024].rearrange("p (s q u) -> p s u q", s=4, q=P, u=2)
+            nc.vector.tensor_copy(out=perm[:].rearrange("p (s u q) -> p s u q", s=4, q=P, u=2), in_=src)
+            return perm
+
+        def transposes(words, starts, step):
             bank = new_bank()
-            words = raw[:].bitcast(F32)
-            for slot in range(4):
-                u, e = slot // 2, slot % 2
-                off = c0 + e * 512 + g * 256 + u
-                nc.tensor.transpose(out=bank[:, slot * P:(slot + 1) * P], in_=words[:, off:off + 255:2], identity=ident[:])
+            for slot, c in enumerate(starts):
+                nc.tensor.transpose(
+                    out=bank[:, slot * P:(slot + 1) * P],
+                    in_=words[:, c:c + step * (P - 1) + 1:step],
+                    identity=ident[:],
+                )
             return bank
+
+        perms = {}
+
+        def sort_x(k):
+            perms[k] = even_odd(xraw[k // 4], (k % 4) * 1024)
 
         lgs = {}
 
-        def lap_turn(a, copies):
-            lg = lgp.tile([P, 2048], BF16, name="lg", tag="lg", align_bytes=64)
-            lgs[a] = lg
+        banks = {}
+
+        def lap_turn(a):
             for g in range(2):
-                bank = transposes(lraw[a], 0, g)
-                dst = lg[:].bitcast(F32)[:, g * 512:(g + 1) * 512].rearrange("q (x u) -> q x u", u=2)
-                copies[g](out=dst, in_=bank[:].rearrange("q (u x) -> q x u", u=2))
+                banks[("l", a, g)] = transposes(lraw[a][:].bitcast(F32), [e * 512 + g * 256 + u for u in range(2) for e in range(2)], 2)
+
+        def lap_out(a, g, copy):
+            if a not in lgs:
+                lg = lgp.tile([P, 2048], BF16, name="lg", tag="lg", align_bytes=64)
+                lgs[a] = lg
+            dst = lgs[a][:].bitcast(F32)[:, g * 512:(g + 1) * 512].rearrange("q (x u) -> q x u", u=2)
+            copy(out=dst, in_=banks[("l", a, g)][:].rearrange("q (u x) -> q x u", u=2))
 
         def lap_quant(a):
             nc.vector.quantize_mx(
@@ -97,21 +115,22 @@ def tile_graph_conv_pa_t_kernel(tc, signal, laplacian, out_0, out_1):
                 in_=lgs[a][:],
             )
 
-        def x_turn(k, copies):
+        def x_turn(k):
             for g in range(2):
-                bank = transposes(xraw[k // 4], (k % 4) * 1024, g)
-                dst = x0g[g][:].bitcast(F32).rearrange("q (f h x u) -> q f h x u", f=2, h=8, x=128, u=2)[:, k // 4]
-                dst = dst[:, :, 32 * (k % 4):32 * (k % 4) + 32, :]
-                copies[g](out=dst, in_=bank[:].rearrange("q (u x h) -> q h x u", u=2, x=32, h=8))
+                banks[("x", k, g)] = transposes(perms[k][:], [e * 512 + g * 256 + u * P for u in range(2) for e in range(2)], 1)
 
-        def x_quant(f, hq):
-            for g in range(2):
-                c = g * N + f * 1024 + hq * 512
-                nc.vector.quantize_mx(
-                    out=x0c[:, c:c + 512].bitcast(FP8X4),
-                    scales=x0s[:, c:c + 512],
-                    in_=x0g[g][:, f * 4096 + hq * 2048:f * 4096 + hq * 2048 + 2048],
-                )
+        def x_out(k, g, copy):
+            dst = x0g[g][:].bitcast(F32).rearrange("q (f h x u) -> q f h x u", f=2, h=8, x=128, u=2)[:, k // 4]
+            dst = dst[:, :, 32 * (k % 4):32 * (k % 4) + 32, :]
+            copy(out=dst, in_=banks[("x", k, g)][:].rearrange("q (u x h) -> q h x u", u=2, x=32, h=8))
+
+        def x_quant(f, hq, g):
+            c = g * N + f * 1024 + hq * 512
+            nc.vector.quantize_mx(
+                out=x0c[:, c:c + 512].bitcast(FP8X4),
+                scales=x0s[:, c:c + 512],
+                in_=x0g[g][:, f * 4096 + hq * 2048:f * 4096 + hq * 2048 + 2048],
+            )
 
         def product(codes, scales, mt, c0, width):
             bank = new_bank()
@@ -182,27 +201,55 @@ def tile_graph_conv_pa_t_kernel(tc, signal, laplacian, out_0, out_1):
         SV = (s_copy, v_copy)
 
         warm(4)
-        lap_turn(0, SV)
-        for k in range(8):
-            x_turn(k, SV)
-            if k == 0:
-                lap_quant(0)
-            if k in (4, 5):
-                x_quant(0, k - 4)
-            if k % 2 == 0:
+        lap_turn(0)
+        sort_x(0)
+        lap_out(0, 0, s_copy)
+        lap_out(0, 1, v_copy)
+        x_turn(0)
+        warm(1)
+        sort_x(1)
+        x_out(0, 0, s_copy)
+        x_out(0, 1, v_copy)
+        lap_quant(0)
+        x_turn(1)
+        warm(1)
+        sort_x(2)
+        x_out(1, 0, s_copy)
+        x_out(1, 1, v_copy)
+        x_turn(2)
+        warm(1)
+        for k in range(3, 8):
+            sort_x(k)
+            for g in range(2):
+                x_out(k - 1, g, s_copy)
+            x_turn(k)
+            if k < 7:
                 warm(1)
-        x_quant(1, 0)
-        lap_turn(1, (s_copy, s_copy))
-        lap_turn(2, SV)
+            if k > 4:
+                x_quant(0, (k - 5) // 2, (k - 5) % 2)
+        x_quant(0, 1, 1)
+        lap_turn(1)
+        x_out(7, 0, s_copy)
+        x_out(7, 1, v_copy)
+        x_quant(1, 0, 0)
+        x_quant(1, 0, 1)
+        lap_out(1, 0, s_copy)
+        lap_out(1, 1, s_copy)
+        lap_turn(2)
         lap_quant(1)
-        x_quant(1, 1)
 
         for t in (0, 1):
             for f in range(2):
                 s1(0, t, f, 0)
             s1_store(0, t, 0)
+        lap_out(2, 0, v_copy)
+        lap_out(2, 1, v_copy)
+        x_quant(1, 1, 0)
+        x_quant(1, 1, 1)
         lap_quant(2)
-        lap_turn(3, SV)
+        lap_turn(3)
+        lap_out(3, 0, s_copy)
+        lap_out(3, 1, v_copy)
         lap_quant(3)
         for t in (2, 3):
             for f in range(2):

@@ -58,7 +58,7 @@ def tile_graph_conv_pa_t_kernel(tc, signal, laplacian, out_0, out_1):
         for a in range(1, 4):
             load_lap(a)
 
-        out_views = [o.rearrange("(gp p t) n -> gp t p n", gp=2, p=P, t=4) for o in (out_0, out_1)]
+        out_rows = [o.rearrange("(gp p t) n -> gp p t n", gp=2, p=P, t=4) for o in (out_0, out_1)]
 
         s_copy = nc.scalar.copy
         v_copy = nc.vector.tensor_copy
@@ -162,10 +162,10 @@ def tile_graph_conv_pa_t_kernel(tc, signal, laplacian, out_0, out_1):
             bank = product(x0c, x0s, 4 * gp + t, f * 1024 + hq * 512, 512)
             copy(out=runs(x1sb[key], t, f), in_=bank[:].rearrange("p (h x) -> p h x", h=4))
 
-        def s1_store(gp, t, hq):
+        def s1_store(gp, t, hq, nt=1):
             nc.sync.dma_start(
-                out=out_views[0][gp, t][:, hq * 1024:(hq + 1) * 1024],
-                in_=x1sb[(gp, hq)][:, t * 1024:(t + 1) * 1024],
+                out=out_rows[0][gp][:, t:t + nt, hq * 1024:(hq + 1) * 1024],
+                in_=x1sb[(gp, hq)][:, t * 1024:(t + nt) * 1024].rearrange("p (t n) -> p t n", t=nt),
             )
 
         def regroup(gp, f, hq, copy=v_copy):
@@ -191,11 +191,11 @@ def tile_graph_conv_pa_t_kernel(tc, signal, laplacian, out_0, out_1):
             else:
                 nc.vector.scalar_tensor_tensor(out=res, in0=src, scalar=2.0, in1=x0t, op0=ALU.mult, op1=ALU.subtract)
 
-        def s2_store(mt, hq, pair, c0=0, c1=1024):
+        def s2_store(mt, hq, pair, nt=1, c0=0, c1=1024):
             t = mt % 4
             nc.sync.dma_start(
-                out=out_views[1][mt // 4, t][:, hq * 1024 + c0:hq * 1024 + c1],
-                in_=pair[:, t * 1024 + c0:t * 1024 + c1],
+                out=out_rows[1][mt // 4][:, t:t + nt, hq * 1024 + c0:hq * 1024 + c1],
+                in_=pair[:, t * 1024:(t + nt) * 1024].rearrange("p (t n) -> p t n", t=nt)[:, :, c0:c1],
             )
 
         SV = (s_copy, v_copy)
@@ -254,11 +254,12 @@ def tile_graph_conv_pa_t_kernel(tc, signal, laplacian, out_0, out_1):
         for t in (2, 3):
             for f in range(2):
                 s1(0, t, f, 0)
-            s1_store(0, t, 0)
+        s1_store(0, 2, 0, 2)
         for t in range(4):
             for f in range(2):
                 s1(0, t, f, 1)
-            s1_store(0, t, 1)
+            if t % 2 == 1:
+                s1_store(0, t - 1, 1, 2)
             if t == 0:
                 regroup(0, 0, 0)
             if t == 2:
@@ -269,7 +270,8 @@ def tile_graph_conv_pa_t_kernel(tc, signal, laplacian, out_0, out_1):
             for t in range(4):
                 for f in range(2):
                     s1(1, t, f, hq)
-                s1_store(1, t, hq)
+                if t % 2 == 1:
+                    s1_store(1, t - 1, hq, 2)
                 if t == 0:
                     regroup(hq, 0, 1 - hq)
                 if t == 2:
@@ -289,12 +291,15 @@ def tile_graph_conv_pa_t_kernel(tc, signal, laplacian, out_0, out_1):
                         for h0 in (0, 2):
                             for f in range(2):
                                 s2(mt, f, hq, pair, False, h0, 2)
-                            s2_store(mt, hq, pair, h0 * 256, h0 * 256 + 512)
+                            s2_store(mt, hq, pair, 1, h0 * 256, h0 * 256 + 512)
                         break
                     for f in range(2):
                         s2(mt, f, hq, pair, i % 4 == 2 and i >= 8 and i < 30)
                         i += 1
-                    s2_store(mt, hq, pair)
+                    if (hq, mt) == (1, 6):
+                        s2_store(mt, hq, pair)
+                    elif t % 2 == 1:
+                        s2_store(mt - 1, hq, pair, 2)
                     if hq == 0 and mt == 3:
                         x1_quant(1, 0, 1)
                     if hq == 0 and mt == 5:

@@ -35,12 +35,12 @@ def tile_graph_conv_pa_t_kernel(tc, signal, laplacian, out_0, out_1):
         lraw = [keep.tile([P, 2048], BF16, name="lraw%d" % a) for a in range(4)]
         xraw = [keep.tile([P, 8192], BF16, name="xraw%d" % i) for i in range(2)]
         x0g = [keep.tile([P, 4 * N], BF16, name="x0g%d" % g, align_bytes=64) for g in range(2)]
-        x0c = keep.tile([P, 2 * N], U32, name="x0c", align_bytes=64)
-        x0s = keep.tile([P, 2 * N], U8, name="x0s", align_bytes=64)
-        x1c = keep.tile([P, 2 * N], U32, name="x1c", align_bytes=64)
-        x1s = keep.tile([P, 2 * N], U8, name="x1s", align_bytes=64)
-        lc = keep.tile([P, 2048], U32, name="lc", align_bytes=64)
-        ls = keep.tile([P, 2048], U8, name="ls", align_bytes=64)
+        x0c = keep.tile([P, 2 * N], U32, name="x0c", align_bytes=256)
+        x0s = keep.tile([P, 2 * N], U8, name="x0s", align_bytes=256)
+        x1c = keep.tile([P, 2 * N], U32, name="x1c", align_bytes=256)
+        x1s = keep.tile([P, 2 * N], U8, name="x1s", align_bytes=256)
+        lc = keep.tile([P, 2048], U32, name="lc", align_bytes=256)
+        ls = keep.tile([P, 2048], U8, name="ls", align_bytes=256)
 
         lap_rows = laplacian.rearrange("(gp p uh e) u -> gp uh p (e u)", gp=2, p=P, uh=2, e=2)
         sig_rows = signal.rearrange("b (h r) v -> (b h) (r v)", h=8, r=16)
@@ -254,12 +254,11 @@ def tile_graph_conv_pa_t_kernel(tc, signal, laplacian, out_0, out_1):
         for t in (2, 3):
             for f in range(2):
                 s1(0, t, f, 0)
-        s1_store(0, 2, 0, 2)
+            s1_store(0, t, 0)
         for t in range(4):
             for f in range(2):
                 s1(0, t, f, 1)
-            if t % 2 == 1:
-                s1_store(0, t - 1, 1, 2)
+            s1_store(0, t, 1)
             if t == 0:
                 regroup(0, 0, 0)
             if t == 2:

from contextlib import ExitStack

import concourse.mybir as mybir
from concourse.masks import make_identity

F32 = mybir.dt.float32
BF16 = mybir.dt.bfloat16
U32 = mybir.dt.uint32
U8 = mybir.dt.uint8
FP8X4 = mybir.dt.float8_e4m3fn_x4
ALU = mybir.AluOpType

P = 128
V = 1024
N = 2048
FLOPS = 2 * 2 * V * V * N


def tile_graph_conv_pa_t_kernel(tc, signal, laplacian, out_0, out_1):
    nc = tc.nc
    with ExitStack() as ctx:
        keep = ctx.enter_context(tc.tile_pool(name="keep", bufs=1))
        big = ctx.enter_context(tc.tile_pool(name="big", bufs=4))
        lgp = ctx.enter_context(tc.tile_pool(name="lgp", bufs=2))
        x1gp = ctx.enter_context(tc.tile_pool(name="x1gp", bufs=3))
        permp = ctx.enter_context(tc.tile_pool(name="permp", bufs=3))
        psum = ctx.enter_context(tc.psum_pool(name="psum", bufs=8))
        ctx.enter_context(tc.manual_schedule())

        ident = keep.tile([P, P], F32, name="ident")
        make_identity(nc, ident[:])
        zeros = keep.tile([P, 512], BF16, name="zeros")
        nc.vector.memset(zeros[:], 0.0)

        lraw = [keep.tile([P, 2048], BF16, name="lraw%d" % a) for a in range(4)]
        xraw = [keep.tile([P, 8192], BF16, name="xraw%d" % i) for i in range(2)]
        x0g = [keep.tile([P, 4 * N], BF16, name="x0g%d" % g, align_bytes=64) for g in range(2)]
        x0c = keep.tile([P, 2 * N], U32, name="x0c", align_bytes=256)
        x0s = keep.tile([P, 2 * N], U8, name="x0s", align_bytes=256)
        x1c = keep.tile([P, 2 * N], U32, name="x1c", align_bytes=256)
        x1s = keep.tile([P, 2 * N], U8, name="x1s", align_bytes=256)
        lc = keep.tile([P, 2048], U32, name="lc", align_bytes=256)
        ls = keep.tile([P, 2048], U8, name="ls", align_bytes=256)

        lap_rows = laplacian.rearrange("(gp p uh e) u -> gp uh p (e u)", gp=2, p=P, uh=2, e=2)
        sig_rows = signal.rearrange("b (h r) v -> (b h) (r v)", h=8, r=16)

        def load_lap(a):
            nc.sync.dma_start(out=lraw[a][:], in_=lap_rows[a // 2, a % 2])

        def load_x(k):
            c = (k % 4) * 2048
            nc.sync.dma_start(out=xraw[k // 4][:, c:c + 2048], in_=sig_rows[:, k * 2048:(k + 1) * 2048])

        load_lap(0)
        for k in range(8):
            load_x(k)
        for a in range(1, 4):
            load_lap(a)

        out_rows = [o.rearrange("(gp p t) n -> gp p t n", gp=2, p=P, t=4) for o in (out_0, out_1)]

        s_copy = nc.scalar.copy
        v_copy = nc.vector.tensor_copy

        def new_bank():
            bank = psum.tile([P, 512], F32, name="bank", tag="bank")
            return bank

        def warm(count):
            bank = new_bank()
            for rep in range(count):
                nc.tensor.matmul(out=bank[:], lhsT=zeros[:, 0:P], rhs=zeros[:], start=True, stop=True)

        def even_odd(raw, c0):
            perm = permp.tile([P, 1024], F32, name="perm", tag="perm")
            src = raw[:].bitcast(F32)[:, c0:c0 + 1024].rearrange("p (s q u) -> p s u q", s=4, q=P, u=2)
            nc.vector.tensor_copy(out=perm[:].rearrange("p (s u q) -> p s u q", s=4, q=P, u=2), in_=src)
            return perm

        def transposes(words, starts, step):
            bank = new_bank()
            for slot, c in enumerate(starts):
                nc.tensor.transpose(
                    out=bank[:, slot * P:(slot + 1) * P],
                    in_=words[:, c:c + step * (P - 1) + 1:step],
                    identity=ident[:],
                )
            return bank

        perms = {}

        def sort_x(k):
            perms[k] = even_odd(xraw[k // 4], (k % 4) * 1024)

        lgs = {}

        banks = {}

        def lap_turn(a):
            for g in range(2):
                banks[("l", a, g)] = transposes(lraw[a][:].bitcast(F32), [e * 512 + g * 256 + u for u in range(2) for e in range(2)], 2)

        def lap_out(a, g, copy):
            if a not in lgs:
                lg = lgp.tile([P, 2048], BF16, name="lg", tag="lg", align_bytes=64)
                lgs[a] = lg
            dst = lgs[a][:].bitcast(F32)[:, g * 512:(g + 1) * 512].rearrange("q (x u) -> q x u", u=2)
            copy(out=dst, in_=banks[("l", a, g)][:].rearrange("q (u x) -> q x u", u=2))

        def lap_quant(a):
            nc.vector.quantize_mx(
                out=lc[:, a * 512:(a + 1) * 512].bitcast(FP8X4),
                scales=ls[:, a * 512:(a + 1) * 512],
                in_=lgs[a][:],
            )

        def x_turn(k):
            for g in range(2):
                banks[("x", k, g)] = transposes(perms[k][:], [e * 512 + g * 256 + u * P for u in range(2) for e in range(2)], 1)

        def x_out(k, g, copy):
            dst = x0g[g][:].bitcast(F32).rearrange("q (f h x u) -> q f h x u", f=2, h=8, x=128, u=2)[:, k // 4]
            dst = dst[:, :, 32 * (k % 4):32 * (k % 4) + 32, :]
            copy(out=dst, in_=banks[("x", k, g)][:].rearrange("q (u x h) -> q h x u", u=2, x=32, h=8))

        def x_quant(f, hq, g):
            c = g * N + f * 1024 + hq * 512
            nc.vector.quantize_mx(
                out=x0c[:, c:c + 512].bitcast(FP8X4),
                scales=x0s[:, c:c + 512],
                in_=x0g[g][:, f * 4096 + hq * 2048:f * 4096 + hq * 2048 + 2048],
            )

        def product(codes, scales, mt, c0, width):
            bank = new_bank()
            for g in range(2):
                w = (mt // 2) * 512 + g * 256 + (mt % 2) * P
                c = g * N + c0
                nc.tensor.matmul_mx(
                    out=bank[:, 0:width],
                    lhsT=lc[:, w:w + P].bitcast(FP8X4),
                    lhsT_scale=ls[:, w:w + P],
                    rhs=codes[:, c:c + width].bitcast(FP8X4),
                    rhs_scale=scales[:, c:c + width],
                    start=(g == 0),
                    stop=(g == 1),
                )
            return bank

        def runs(tile, t, f):
            return tile[:, t * 1024:(t + 1) * 1024].rearrange("p (h f x) -> p f h x", h=4, f=2, x=P)[:, f]

        x1sb = {}
        x1g = {}

        def s1(gp, t, f, hq, copy=s_copy):
            key = (gp, hq)
            if key not in x1sb:
                pair = big.tile([P, 4096], F32, name="pair", tag="big")
                x1sb[key] = pair
            bank = product(x0c, x0s, 4 * gp + t, f * 1024 + hq * 512, 512)
            copy(out=runs(x1sb[key], t, f), in_=bank[:].rearrange("p (h x) -> p h x", h=4))

        def s1_store(gp, t, hq, nt=1):
            nc.sync.dma_start(
                out=out_rows[0][gp][:, t:t + nt, hq * 1024:(hq + 1) * 1024],
                in_=x1sb[(gp, hq)][:, t * 1024:(t + nt) * 1024].rearrange("p (t n) -> p t n", t=nt),
            )

        def regroup(gp, f, hq, copy=v_copy):
            xg = x1gp.tile([P, 2048], BF16, name="xg", tag="xg", align_bytes=64)
            x1g[(gp, f, hq)] = xg
            src = x1sb[(gp, hq)][:].rearrange("p (t h f c i) -> p f h c t i", t=4, h=4, f=2, c=32, i=4)[:, f]
            copy(out=xg[:].rearrange("p (h c i t) -> p h c t i", h=4, c=32, i=4, t=4), in_=src)

        def x1_quant(gp, f, hq):
            c = gp * N + f * 1024 + hq * 512
            nc.vector.quantize_mx(out=x1c[:, c:c + 512].bitcast(FP8X4), scales=x1s[:, c:c + 512], in_=x1g[(gp, f, hq)][:])

        def s2(mt, f, hq, pair, scalar_path, h0=0, nh=4):
            c = f * 1024 + hq * 512 + h0 * P
            bank = product(x1c, x1s, mt, c, nh * P)
            src = bank[:, 0:nh * P].rearrange("p (h x) -> p h x", h=nh)
            x0t = x0g[mt // 4][:].rearrange("q (n t) -> q n t", t=4)[:, c:c + nh * P, mt % 4]
            x0t = x0t.rearrange("q (h x) -> q h x", h=nh)
            res = runs(pair, mt % 4, f)[:, h0:h0 + nh]
            if scalar_path:
                nc.scalar.mul(out=res, in_=src, mul=2.0)
                nc.gpsimd.tensor_tensor(out=res, in0=res, in1=x0t, op=ALU.subtract)
            else:
                nc.vector.scalar_tensor_tensor(out=res, in0=src, scalar=2.0, in1=x0t, op0=ALU.mult, op1=ALU.subtract)

        def s2_store(mt, hq, pair, nt=1, c0=0, c1=1024):
            t = mt % 4
            nc.sync.dma_start(
                out=out_rows[1][mt // 4][:, t:t + nt, hq * 1024 + c0:hq * 1024 + c1],
                in_=pair[:, t * 1024:(t + nt) * 1024].rearrange("p (t n) -> p t n", t=nt)[:, :, c0:c1],
            )

        SV = (s_copy, v_copy)

        warm(4)
        lap_turn(0)
        sort_x(0)
        lap_out(0, 0, s_copy)
        lap_out(0, 1, v_copy)
        x_turn(0)
        warm(1)
        sort_x(1)
        x_out(0, 0, s_copy)
        x_out(0, 1, v_copy)
        lap_quant(0)
        x_turn(1)
        warm(1)
        sort_x(2)
        x_out(1, 0, s_copy)
        x_out(1, 1, v_copy)
        x_turn(2)
        warm(1)
        for k in range(3, 8):
            sort_x(k)
            for g in range(2):
                x_out(k - 1, g, s_copy)
            x_turn(k)
            if k < 7:
                warm(1)
            if k > 4:
                x_quant(0, (k - 5) // 2, (k - 5) % 2)
        x_quant(0, 1, 1)
        lap_turn(1)
        x_out(7, 0, s_copy)
        x_out(7, 1, v_copy)
        x_quant(1, 0, 0)
        x_quant(1, 0, 1)
        lap_out(1, 0, s_copy)
        lap_out(1, 1, s_copy)
        lap_turn(2)
        lap_quant(1)

        for t in (0, 1):
            for f in range(2):
                s1(0, t, f, 0)
            s1_store(0, t, 0)
        lap_out(2, 0, v_copy)
        lap_out(2, 1, v_copy)
        x_quant(1, 1, 0)
        x_quant(1, 1, 1)
        lap_quant(2)
        lap_turn(3)
        lap_out(3, 0, s_copy)
        lap_out(3, 1, v_copy)
        lap_quant(3)
        for t in (2, 3):
            for f in range(2):
                s1(0, t, f, 0)
            s1_store(0, t, 0)
        for t in range(4):
            for f in range(2):
                s1(0, t, f, 1)
            s1_store(0, t, 1)
            if t == 0:
                regroup(0, 0, 0)
            if t == 2:
                regroup(0, 1, 0)
                x1_quant(0, 0, 0)
        x1_quant(0, 1, 0)
        for hq in range(2):
            for t in range(4):
                for f in range(2):
                    s1(1, t, f, hq)
                if t % 2 == 1:
                    s1_store(1, t - 1, hq, 2)
                if t == 0:
                    regroup(hq, 0, 1 - hq)
                if t == 2:
                    regroup(hq, 1, 1 - hq)
                    x1_quant(hq, 0, 1 - hq)
            x1_quant(hq, 1, 1 - hq)

        regroup(1, 0, 1, s_copy)
        regroup(1, 1, 1, s_copy)
        i = 0
        for hq in range(2):
            for gp in range(2):
                pair = big.tile([P, 4096], F32, name="pair", tag="big")
                for t in range(4):
                    mt = 4 * gp + t
                    if (hq, mt) == (1, 7):
                        for h0 in (0, 2):
                            for f in range(2):
                                s2(mt, f, hq, pair, False, h0, 2)
                            s2_store(mt, hq, pair, 1, h0 * 256, h0 * 256 + 512)
                        break
                    for f in range(2):
                        s2(mt, f, hq, pair, i % 4 == 2 and i >= 8 and i < 30)
                        i += 1
                    if (hq, mt) == (1, 6):
                        s2_store(mt, hq, pair)
                    elif t % 2 == 1:
                        s2_store(mt - 1, hq, pair, 2)
                    if hq == 0 and mt == 3:
                        x1_quant(1, 0, 1)
                    if hq == 0 and mt == 5:
                        x1_quant(1, 1, 1)
